import numpy as np
import ml_dtypes


def mxq(x, axis, fmt="e4m3"):
    dtype, down = {"e4m3": (ml_dtypes.float8_e4m3fn, 7), "e5m2": (ml_dtypes.float8_e5m2, 14)}[fmt]
    v = np.moveaxis(np.asarray(x, np.float32).astype(ml_dtypes.bfloat16).astype(np.float64), axis, -1)
    blocks = v.reshape(v.shape[:-1] + (-1, 32))
    amax = np.abs(blocks).max(-1, keepdims=True)
    byte = np.maximum(np.where(amax > 0, np.frexp(amax)[1] - 1 + 127, 0) - down, 1)
    scale = np.exp2(byte - 127.0)
    codes = (blocks / scale).astype(np.float32).astype(dtype).astype(np.float64)
    return np.moveaxis((codes * scale).reshape(v.shape), -1, axis)


WIDE = False


def mx_kscale(k):
    if not WIDE:
        return np.ones(k)
    levels = np.array([30, -30])
    if k % 512:
        return np.exp2(np.random.permutation(np.resize(levels, k // 32))).repeat(32)
    a = np.empty((k // 512, 16))
    for p in range(k // 512):
        a[p, :8] = np.random.permutation(np.resize(levels, 8))
        for g in range(8):
            far = levels[np.abs(levels - a[p, g]) >= 10]
            a[p, g + 8] = far[np.random.randint(len(far))]
    return np.exp2(a.ravel()).repeat(32)


BF16 = ml_dtypes.bfloat16


def bf(x):
    return np.asarray(x, np.float32).astype(BF16)


def f64(x):
    return np.asarray(x).astype(np.float64)


E2M1 = np.array([0.0, 0.5, 1.0, 1.5, 2.0, 3.0, 4.0, 6.0, -0.0, -0.5, -1.0, -1.5, -2.0, -3.0, -4.0, -6.0])


def pack_weight(w, fmt):
    k, n = w.shape
    w = f64(bf(w)).reshape(k // 32, 32, n)
    amax = np.abs(w).max(1)
    if fmt == "e4m3":
        byte = np.frexp(amax)[1] - 1 + 127 - 7
    else:
        mant, ex = np.frexp(amax / 6.0)
        byte = np.where(mant > 0.5, ex, ex - 1) + 127
    byte = np.clip(np.where(amax > 0, byte, 1), 1, 254)
    scaled = (w * np.exp2(127.0 - byte)[:, None, :]).reshape(k, n).astype(np.float32)
    by_word = np.ascontiguousarray(scaled.reshape(k // 512, 128, 4, n).transpose(0, 1, 3, 2))
    if fmt == "e4m3":
        words = by_word.astype(ml_dtypes.float8_e4m3fn).view(np.uint8)
    else:
        c = by_word.astype(ml_dtypes.float4_e2m1fn).view(np.uint8) & 0xF
        words = c[..., 0::2] | (c[..., 1::2] << 4)
    return np.ascontiguousarray(words), np.ascontiguousarray(byte.astype(np.uint8).reshape(k // 512, 16, n))


def unpack_weight(words, scales, fmt):
    g, p, n, _ = words.shape
    if fmt == "e4m3":
        vals = np.ascontiguousarray(words).view(ml_dtypes.float8_e4m3fn).astype(np.float64)
    else:
        nib = np.empty((g, p, n, 4), np.uint8)
        nib[..., 0::2] = words & 0xF
        nib[..., 1::2] = words >> 4
        vals = E2M1[nib]
    vals = vals * np.repeat(np.exp2(scales.astype(np.float64) - 127.0), 8, axis=1)[..., None]
    return vals.transpose(0, 1, 3, 2).reshape(g * 512, n)

def pack4(w):
    words, scales = pack_weight(w, "e2m1")
    return words.reshape(words.shape[0], 128, -1), scales


def unpack4(words, scales):
    return unpack_weight(words.reshape(words.shape[0], 128, -1, 2), scales, "e2m1")


B, T, D, H, QB = 1, 1024, 1024, 8, 512
DH = D // H
HP = H // 2
EPS = 1e-6
ROPE_BASE = 10000.0


def rmsnorm(u):
    return u / np.sqrt(np.mean(u * u, axis=-1, keepdims=True) + EPS)


def rope_tables():
    inv_freq = 1.0 / ROPE_BASE ** (np.arange(0, DH, 2) / DH)
    freqs = np.arange(T)[:, None] * inv_freq[None, :]
    return np.cos(freqs), np.sin(freqs)


def apply_rotary(u, cos, sin):
    d = DH // 2
    u1, u2 = u[..., :d], u[..., d:]
    c = cos[None, :, None, :]
    s = sin[None, :, None, :]
    return np.concatenate([u1 * c + u2 * s, -u1 * s + u2 * c], axis=-1)


def setup_inputs():
    s = mx_kscale(D)
    hidden_states = bf(np.random.standard_normal((B, T, D)) * s)
    words, scales = pack4(np.random.standard_normal((D, 3 * D)) / np.sqrt(D) / s[:, None])
    return {"hidden_states": hidden_states,
            "W_qkv_words": words,
            "W_qkv_scales": scales}


def reference(hidden_states, W_qkv_words, W_qkv_scales):
    x = f64(hidden_states).reshape(B * T, D)
    qkv = mxq(x, 1, "e5m2") @ unpack4(W_qkv_words, W_qkv_scales)
    qkv = qkv.reshape(B, T, H, 3 * DH)
    q = qkv[..., :DH]
    k = qkv[..., DH:2 * DH]
    v = qkv[..., 2 * DH:]
    v = v.reshape(B, T, HP, 2 * DH)
    cos, sin = rope_tables()
    q = apply_rotary(rmsnorm(q), cos, sin)
    k = apply_rotary(rmsnorm(k), cos, sin)
    return q, k, v

@@ -1,0 +1,237 @@
+import math
+from contextlib import ExitStack
+
+import concourse.mybir as mybir
+from concourse.masks import make_identity
+
+T, D, H = 1024, 1024, 8
+DH = 128
+HALF = DH // 2
+EPS = 1e-6
+ROPE_BASE = 10000.0
+FLOPS = 2 * T * D * 3 * D
+
+F32 = mybir.dt.float32
+BF16 = mybir.dt.bfloat16
+I32 = mybir.dt.int32
+U32 = mybir.dt.uint32
+U8 = mybir.dt.uint8
+E5M2X4 = mybir.dt.float8_e5m2_x4
+E2M1X4 = mybir.dt.float4_e2m1fn_x4
+ALU = mybir.AluOpType
+ACT = mybir.ActivationFunctionType
+
+P = 128
+PASSES = D // 512
+TILES = T // P
+BANK = 512
+GROUP_HEADS = 4
+GROUP_COLS = GROUP_HEADS * 3 * DH
+GROUP_BANKS = GROUP_COLS // BANK
+GROUPS = H // GROUP_HEADS
+NORMED = 2 * GROUP_HEADS
+
+
+def tile_mixerdiffattention_pa_kernel(tc, hidden_states, W_qkv_words, W_qkv_scales, out_0, out_1, out_2):
+    nc = tc.nc
+    x_hbm = hidden_states.rearrange("b t d -> (b t) d")
+    q_hbm = out_0.rearrange("b t h d -> (b t) (h d)")
+    k_hbm = out_1.rearrange("b t h d -> (b t) (h d)")
+    v_hbm = out_2.rearrange("b t h d -> (b t) (h d)")
+
+    with ExitStack() as ctx:
+        keep = ctx.enter_context(tc.tile_pool(name="keep", bufs=1))
+        work = ctx.enter_context(tc.tile_pool(name="work", bufs=3))
+        psum = ctx.enter_context(tc.psum_pool(name="psum", bufs=8))
+        ctx.enter_context(tc.manual_schedule())
+
+        x_sb = [keep.tile([P, D], BF16, name="x%d" % i, align_bytes=64) for i in range(TILES)]
+        w_sb = [keep.tile([P, PASSES, 2 * BANK], U8, name="w%d" % c, align_bytes=64) for c in range(GROUPS * GROUP_BANKS)]
+        w_scale = [keep.tile([P, PASSES, GROUP_COLS], U8, name="ws%d" % g, align_bytes=64) for g in range(GROUPS)]
+        ident = keep.tile([P, P], F32, align_bytes=64)
+        pos = keep.tile([P, TILES], F32)
+        low = keep.tile([P, TILES, 8], F32)
+        turns = keep.tile([P, TILES, HALF], F32)
+        whole = keep.tile([P, 2, TILES * HALF], I32)
+        frac = keep.tile([P, 2, TILES, HALF], F32)
+        table = keep.tile([P, TILES, 2, 2, HALF], F32)
+
+        def load_x(i):
+            nc.sync.dma_start(out=x_sb[i][:], in_=x_hbm[i * P : (i + 1) * P, :])
+
+        def load_words(c):
+            src = W_qkv_words[:, :, 2 * BANK * c : 2 * BANK * (c + 1)].rearrange("g p n -> p g n")
+            nc.sync.dma_start(out=w_sb[c][:].bitcast(I32), in_=src.bitcast(I32))
+
+        def load_scales(g):
+            for quad in range(4):
+                src = W_qkv_scales[:, 4 * quad : 4 * quad + 4, GROUP_COLS * g : GROUP_COLS * (g + 1)]
+                nc.sync.dma_start(
+                    out=w_scale[g][32 * quad : 32 * quad + 4, :, :].bitcast(I32),
+                    in_=src.rearrange("g r n -> r g n").bitcast(I32),
+                )
+
+        nc.gpsimd.iota(pos[:], pattern=[[P, TILES]], base=0, channel_multiplier=1, allow_small_or_imprecise_dtypes=True)
+        make_identity(nc, ident[:])
+        for g in range(GROUPS):
+            nc.vector.memset(w_scale[g][:].bitcast(I32), 0)
+
+        load_x(0)
+        load_x(1)
+        load_words(0)
+        load_scales(0)
+        load_words(1)
+        load_words(2)
+        load_scales(1)
+        for c in range(GROUP_BANKS, GROUPS * GROUP_BANKS):
+            load_words(c)
+        for i in range(2, TILES):
+            load_x(i)
+
+        for b in range(8):
+            nc.vector.tensor_scalar(
+                out=low[:, :, b], in0=pos[:], scalar1=ROPE_BASE ** (-b / HALF) / (2 * math.pi), scalar2=None, op0=ALU.mult
+            )
+        for m in range(HALF // 8):
+            nc.vector.tensor_scalar(
+                out=turns[:, :, 8 * m : 8 * m + 8], in0=low[:], scalar1=ROPE_BASE ** (-8 * m / HALF), scalar2=None, op0=ALU.mult
+            )
+        turns_flat = turns[:].rearrange("p a j -> p (a j)")
+        shifts = (0.25, 0.0)
+        for w in range(2):
+            nc.vector.tensor_scalar(out=whole[:, w, :], in0=turns_flat, scalar1=shifts[w], scalar2=None, op0=ALU.add)
+        for w in range(2):
+            nc.vector.scalar_tensor_tensor(
+                out=frac[:, w, :, :].rearrange("p a j -> p (a j)"),
+                in0=turns_flat,
+                scalar=shifts[w],
+                in1=whole[:, w, :],
+                op0=ALU.add,
+                op1=ALU.subtract,
+            )
+
+        grouped = {}
+        codes = {}
+        scales = {}
+        banks = {}
+        rstd = {}
+
+        def transpose_x(i, copy_out):
+            words = x_sb[i][:].bitcast(F32)
+            xt = psum.tile([P, BANK], F32, name="bank")
+            xt4 = xt[:].rearrange("p (g u r) -> p g u r", g=PASSES, u=2)
+            for g in range(PASSES):
+                for u in range(2):
+                    nc.tensor.transpose(xt4[:, g, u, :], words[:, 256 * g + u : 256 * (g + 1) : 2], ident[:])
+            grouped[i] = work.tile([P, D], BF16, name="grouped", align_bytes=64)
+            copy_out(
+                out=grouped[i][:].bitcast(F32).rearrange("p (g r u) -> p g r u", g=PASSES, u=2),
+                in_=xt4.rearrange("p g u r -> p g r u"),
+            )
+
+        def quantize_x(i):
+            codes[i] = work.tile([P, PASSES * P], U32, name="codes", align_bytes=64)
+            scales[i] = work.tile([P, PASSES * P], U8, name="scales", align_bytes=64)
+            nc.vector.quantize_mx(out=codes[i][:].bitcast(E5M2X4), scales=scales[i][:], in_=grouped[i][:])
+
+        def inverse_rms(dst, sums):
+            nc.scalar.activation(out=dst, in_=sums, func=ACT.Abs_reciprocal_sqrt, scale=1.0 / DH, bias=EPS)
+
+        def project(step):
+            i, g = divmod(step, GROUPS)
+            sums = work.tile([P, NORMED], F32, name="sums")
+            squares = work.tile([P, NORMED, DH], F32, name="squares")
+            v_sb = work.tile([P, GROUP_HEADS, DH], F32, name="v_sb")
+            rstd[step] = work.tile([P, NORMED], F32, name="rstd")
+            for b in range(GROUP_BANKS):
+                acc = psum.tile([P, BANK], F32, name="bank")
+                banks[step, b] = acc
+                for s in range(PASSES):
+                    nc.tensor.matmul_mx(
+                        out=acc[:],
+                        lhsT=codes[i][:, P * s : P * (s + 1)].bitcast(E5M2X4),
+                        lhsT_scale=scales[i][:, P * s : P * (s + 1)],
+                        rhs=w_sb[GROUP_BANKS * g + b][:, s, :].bitcast(E2M1X4),
+                        rhs_scale=w_scale[g][:, s, BANK * b : BANK * (b + 1)],
+                        start=(s == 0),
+                        stop=(s == PASSES - 1),
+                    )
+                blocks = acc[:].rearrange("p (n d) -> p n d", d=DH)
+                v_slots = []
+                units = []
+                for n in range(4):
+                    head, kind = divmod(4 * b + n, 3)
+                    if kind == 2:
+                        v_slots.append((n, head))
+                    else:
+                        unit = GROUP_HEADS * kind + head
+                        units.append(unit)
+                        nc.scalar.activation(
+                            out=squares[:, unit, :], in_=blocks[:, n, :], func=ACT.Square, accum_out=sums[:, unit : unit + 1]
+                        )
+                n0, head0 = v_slots[0]
+                nc.scalar.copy(out=v_sb[:, head0 : head0 + len(v_slots), :], in_=blocks[:, n0:4:3, :])
+                if step == 0:
+                    for unit in units:
+                        inverse_rms(rstd[step][:, unit : unit + 1], sums[:, unit : unit + 1])
+            if step > 0:
+                inverse_rms(rstd[step][:], sums[:])
+            cols = slice(GROUP_HEADS * DH * g, GROUP_HEADS * DH * (g + 1))
+            nc.sync.dma_start(out=v_hbm[i * P : (i + 1) * P, cols], in_=v_sb[:].rearrange("p h d -> p (h d)"))
+
+        def combine(engine, rotated, prods, units):
+            engine.tensor_tensor(
+                out=rotated[:, units, 0:HALF], in0=prods[:, units, 0, 0:HALF], in1=prods[:, units, 1, HALF:DH], op=ALU.add
+            )
+            engine.tensor_tensor(
+                out=rotated[:, units, HALF:DH], in0=prods[:, units, 0, HALF:DH], in1=prods[:, units, 1, 0:HALF], op=ALU.subtract
+            )
+
+        def rotate(step):
+            i, g = divmod(step, GROUPS)
+            prods = work.tile([P, NORMED, 2, DH], F32, name="prods")
+            rotated = work.tile([P, NORMED, DH], F32, name="rotated")
+            for b in range(GROUP_BANKS):
+                blocks = banks[step, b][:].rearrange("p (n d) -> p n d", d=DH)
+                for n in range(4):
+                    head, kind = divmod(4 * b + n, 3)
+                    if kind != 2:
+                        unit = GROUP_HEADS * kind + head
+                        nc.vector.scalar_tensor_tensor(
+                            out=prods[:, unit, :, :],
+                            in0=blocks[:, n : n + 1, :].to_broadcast([P, 2, DH]),
+                            scalar=rstd[step][:, unit : unit + 1],
+                            in1=table[:, i, :, :, :].rearrange("p w c j -> p w (c j)"),
+                            op0=ALU.mult,
+                            op1=ALU.mult,
+                        )
+            cols = slice(GROUP_HEADS * DH * g, GROUP_HEADS * DH * (g + 1))
+            rows = slice(i * P, (i + 1) * P)
+            last = step == TILES * GROUPS - 1
+            if not last:
+                combine(nc.gpsimd, rotated, prods, slice(0, NORMED))
+            for kind, dst in enumerate((q_hbm, k_hbm)):
+                units = slice(GROUP_HEADS * kind, GROUP_HEADS * (kind + 1))
+                if last:
+                    combine(nc.vector, rotated, prods, units)
+                nc.sync.dma_start(out=dst[rows, cols], in_=rotated[:, units, :].rearrange("p h d -> p (h d)"))
+
+        transpose_x(0, nc.scalar.copy)
+        quantize_x(0)
+        for w in range(2):
+            nc.scalar.activation(out=table[:, :, w, 0, :], in_=frac[:, w, :, :], func=ACT.Sin, scale=2 * math.pi)
+        transpose_x(1, nc.vector.tensor_copy)
+        nc.vector.tensor_copy(out=table[:, :, :, 1, :], in_=table[:, :, :, 0, :])
+        quantize_x(1)
+
+        steps = TILES * GROUPS
+        project(0)
+        for step in range(steps):
+            if step + 1 < steps:
+                project(step + 1)
+            i, g = divmod(step, GROUPS)
+            if g == 0 and i + 2 < TILES:
+                transpose_x(i + 2, nc.scalar.copy)
+            rotate(step)
+            if g == GROUPS - 1 and i + 2 < TILES:
+                quantize_x(i + 2)

@@ -143,6 +143,7 @@ def tile_mixerdiffattention_pa_kernel(tc, hidden_states, W_qkv_words, W_qkv_scal
             squares = work.tile([P, NORMED, DH], F32, name="squares")
             v_sb = work.tile([P, GROUP_HEADS, DH], F32, name="v_sb")
             rstd[step] = work.tile([P, NORMED], F32, name="rstd")
+            order = []
             for b in range(GROUP_BANKS):
                 acc = psum.tile([P, BANK], F32, name="bank")
                 banks[step, b] = acc
@@ -158,39 +159,41 @@ def tile_mixerdiffattention_pa_kernel(tc, hidden_states, W_qkv_words, W_qkv_scal
                     )
                 blocks = acc[:].rearrange("p (n d) -> p n d", d=DH)
                 v_slots = []
-                units = []
+                first = len(order)
                 for n in range(4):
                     head, kind = divmod(4 * b + n, 3)
                     if kind == 2:
                         v_slots.append((n, head))
                     else:
                         unit = GROUP_HEADS * kind + head
-                        units.append(unit)
+                        slot = len(order)
+                        order.append(unit)
                         nc.scalar.activation(
-                            out=squares[:, unit, :], in_=blocks[:, n, :], func=ACT.Square, accum_out=sums[:, unit : unit + 1]
+                            out=squares[:, slot, :], in_=blocks[:, n, :], func=ACT.Square, accum_out=sums[:, slot : slot + 1]
                         )
                 n0, head0 = v_slots[0]
                 nc.scalar.copy(out=v_sb[:, head0 : head0 + len(v_slots), :], in_=blocks[:, n0:4:3, :])
                 if step == 0:
-                    for unit in units:
-                        inverse_rms(rstd[step][:, unit : unit + 1], sums[:, unit : unit + 1])
+                    inverse_rms(rstd[step][:, first : len(order)], sums[:, first : len(order)])
             if step > 0:
                 inverse_rms(rstd[step][:], sums[:])
             cols = slice(GROUP_HEADS * DH * g, GROUP_HEADS * DH * (g + 1))
             nc.sync.dma_start(out=v_hbm[i * P : (i + 1) * P, cols], in_=v_sb[:].rearrange("p h d -> p (h d)"))
 
         def combine(engine, rotated, prods, units):
+            halves = prods[:, units, :, :].rearrange("p u w (c j) -> p u w c j", c=2)
             engine.tensor_tensor(
-                out=rotated[:, units, 0:HALF], in0=prods[:, units, 0, 0:HALF], in1=prods[:, units, 1, HALF:DH], op=ALU.add
-            )
-            engine.tensor_tensor(
-                out=rotated[:, units, HALF:DH], in0=prods[:, units, 0, HALF:DH], in1=prods[:, units, 1, 0:HALF], op=ALU.subtract
+                out=rotated[:, units, :].rearrange("p u (c j) -> p u c j", c=2),
+                in0=halves[:, :, 0, :, :],
+                in1=halves[:, :, 1, ::-1, :],
+                op=ALU.add,
             )
 
         def rotate(step):
             i, g = divmod(step, GROUPS)
             prods = work.tile([P, NORMED, 2, DH], F32, name="prods")
             rotated = work.tile([P, NORMED, DH], F32, name="rotated")
+            slot = 0
             for b in range(GROUP_BANKS):
                 blocks = banks[step, b][:].rearrange("p (n d) -> p n d", d=DH)
                 for n in range(4):
@@ -200,11 +203,12 @@ def tile_mixerdiffattention_pa_kernel(tc, hidden_states, W_qkv_words, W_qkv_scal
                         nc.vector.scalar_tensor_tensor(
                             out=prods[:, unit, :, :],
                             in0=blocks[:, n : n + 1, :].to_broadcast([P, 2, DH]),
-                            scalar=rstd[step][:, unit : unit + 1],
+                            scalar=rstd[step][:, slot : slot + 1],
                             in1=table[:, i, :, :, :].rearrange("p w c j -> p w (c j)"),
                             op0=ALU.mult,
                             op1=ALU.mult,
                         )
+                        slot += 1
             cols = slice(GROUP_HEADS * DH * g, GROUP_HEADS * DH * (g + 1))
             rows = slice(i * P, (i + 1) * P)
             last = step == TILES * GROUPS - 1
@@ -216,12 +220,15 @@ def tile_mixerdiffattention_pa_kernel(tc, hidden_states, W_qkv_words, W_qkv_scal
                     combine(nc.vector, rotated, prods, units)
                 nc.sync.dma_start(out=dst[rows, cols], in_=rotated[:, units, :].rearrange("p h d -> p (h d)"))
 
-        transpose_x(0, nc.scalar.copy)
-        quantize_x(0)
         for w in range(2):
-            nc.scalar.activation(out=table[:, :, w, 0, :], in_=frac[:, w, :, :], func=ACT.Sin, scale=2 * math.pi)
+            nc.scalar.activation(out=table[:, :, w, 1, :], in_=frac[:, w, :, :], func=ACT.Sin, scale=2 * math.pi)
+        transpose_x(0, nc.vector.tensor_copy)
+        nc.vector.tensor_copy(out=table[:, :, 0, 0, :], in_=table[:, :, 0, 1, :])
+        quantize_x(0)
         transpose_x(1, nc.vector.tensor_copy)
-        nc.vector.tensor_copy(out=table[:, :, :, 1, :], in_=table[:, :, :, 0, :])
+        nc.vector.tensor_scalar(
+            out=table[:, :, 1, 0, :], in0=table[:, :, 1, 1, :], scalar1=-1.0, scalar2=None, op0=ALU.mult
+        )
         quantize_x(1)
 
         steps = TILES * GROUPS

@@ -79,11 +79,9 @@ def tile_mixerdiffattention_pa_kernel(tc, hidden_states, W_qkv_words, W_qkv_scal
         load_x(0)
         load_x(1)
         load_words(0)
-        load_scales(0)
-        load_words(1)
-        load_words(2)
-        load_scales(1)
-        for c in range(GROUP_BANKS, GROUPS * GROUP_BANKS):
+        for g in range(GROUPS):
+            load_scales(g)
+        for c in range(1, GROUPS * GROUP_BANKS):
             load_words(c)
         for i in range(2, TILES):
             load_x(i)
@@ -144,6 +142,7 @@ def tile_mixerdiffattention_pa_kernel(tc, hidden_states, W_qkv_words, W_qkv_scal
             v_sb = work.tile([P, GROUP_HEADS, DH], F32, name="v_sb")
             rstd[step] = work.tile([P, NORMED], F32, name="rstd")
             order = []
+            by_bank = step in (0, TILES * GROUPS - 1)
             for b in range(GROUP_BANKS):
                 acc = psum.tile([P, BANK], F32, name="bank")
                 banks[step, b] = acc
@@ -173,9 +172,9 @@ def tile_mixerdiffattention_pa_kernel(tc, hidden_states, W_qkv_words, W_qkv_scal
                         )
                 n0, head0 = v_slots[0]
                 nc.scalar.copy(out=v_sb[:, head0 : head0 + len(v_slots), :], in_=blocks[:, n0:4:3, :])
-                if step == 0:
+                if by_bank:
                     inverse_rms(rstd[step][:, first : len(order)], sums[:, first : len(order)])
-            if step > 0:
+            if not by_bank:
                 inverse_rms(rstd[step][:], sums[:])
             cols = slice(GROUP_HEADS * DH * g, GROUP_HEADS * DH * (g + 1))
             nc.sync.dma_start(out=v_hbm[i * P : (i + 1) * P, cols], in_=v_sb[:].rearrange("p h d -> p (h d)"))

@@ -114,6 +114,13 @@ def tile_mixerdiffattention_pa_kernel(tc, hidden_states, W_qkv_words, W_qkv_scal
         banks = {}
         rstd = {}
 
+        warm_bank = psum.tile([P, BANK], F32, name="bank")
+        warm_act = keep.tile([P, 1], F32)
+
+        def warm_tensor():
+            for n in range(3):
+                nc.tensor.matmul(warm_bank[:, P * n : P * (n + 1)], lhsT=ident[:], rhs=ident[:], start=True, stop=True)
+
         def transpose_x(i, copy_out):
             words = x_sb[i][:].bitcast(F32)
             xt = psum.tile([P, BANK], F32, name="bank")
@@ -221,6 +228,8 @@ def tile_mixerdiffattention_pa_kernel(tc, hidden_states, W_qkv_words, W_qkv_scal
 
         for w in range(2):
             nc.scalar.activation(out=table[:, :, w, 1, :], in_=frac[:, w, :, :], func=ACT.Sin, scale=2 * math.pi)
+        inverse_rms(warm_act[:], pos[:, 0:1])
+        warm_tensor()
         transpose_x(0, nc.vector.tensor_copy)
         nc.vector.tensor_copy(out=table[:, :, 0, 0, :], in_=table[:, :, 0, 1, :])
         quantize_x(0)
@@ -229,6 +238,7 @@ def tile_mixerdiffattention_pa_kernel(tc, hidden_states, W_qkv_words, W_qkv_scal
             out=table[:, :, 1, 0, :], in0=table[:, :, 1, 1, :], scalar1=-1.0, scalar2=None, op0=ALU.mult
         )
         quantize_x(1)
+        warm_tensor()
 
         steps = TILES * GROUPS
         project(0)

import math
from contextlib import ExitStack

import concourse.mybir as mybir
from concourse.masks import make_identity

T, D, H = 1024, 1024, 8
DH = 128
HALF = DH // 2
EPS = 1e-6
ROPE_BASE = 10000.0
FLOPS = 2 * T * D * 3 * D

F32 = mybir.dt.float32
BF16 = mybir.dt.bfloat16
I32 = mybir.dt.int32
U32 = mybir.dt.uint32
U8 = mybir.dt.uint8
E5M2X4 = mybir.dt.float8_e5m2_x4
E2M1X4 = mybir.dt.float4_e2m1fn_x4
ALU = mybir.AluOpType
ACT = mybir.ActivationFunctionType

P = 128
PASSES = D // 512
TILES = T // P
BANK = 512
GROUP_HEADS = 4
GROUP_COLS = GROUP_HEADS * 3 * DH
GROUP_BANKS = GROUP_COLS // BANK
GROUPS = H // GROUP_HEADS
NORMED = 2 * GROUP_HEADS


def tile_mixerdiffattention_pa_kernel(tc, hidden_states, W_qkv_words, W_qkv_scales, out_0, out_1, out_2):
    nc = tc.nc
    x_hbm = hidden_states.rearrange("b t d -> (b t) d")
    q_hbm = out_0.rearrange("b t h d -> (b t) (h d)")
    k_hbm = out_1.rearrange("b t h d -> (b t) (h d)")
    v_hbm = out_2.rearrange("b t h d -> (b t) (h d)")

    with ExitStack() as ctx:
        keep = ctx.enter_context(tc.tile_pool(name="keep", bufs=1))
        work = ctx.enter_context(tc.tile_pool(name="work", bufs=3))
        psum = ctx.enter_context(tc.psum_pool(name="psum", bufs=8))
        ctx.enter_context(tc.manual_schedule())

        x_sb = [keep.tile([P, D], BF16, name="x%d" % i, align_bytes=64) for i in range(TILES)]
        w_sb = [keep.tile([P, PASSES, 2 * BANK], U8, name="w%d" % c, align_bytes=64) for c in range(GROUPS * GROUP_BANKS)]
        w_scale = [keep.tile([P, PASSES, GROUP_COLS], U8, name="ws%d" % g, align_bytes=64) for g in range(GROUPS)]
        ident = keep.tile([P, P], F32, align_bytes=64)
        pos = keep.tile([P, TILES], F32)
        low = keep.tile([P, TILES, 8], F32)
        turns = keep.tile([P, TILES, HALF], F32)
        whole = keep.tile([P, 2, TILES * HALF], I32)
        frac = keep.tile([P, 2, TILES, HALF], F32)
        table = keep.tile([P, TILES, 2, 2, HALF], F32)

        def load_x(i):
            nc.sync.dma_start(out=x_sb[i][:], in_=x_hbm[i * P : (i + 1) * P, :])

        def load_words(c):
            src = W_qkv_words[:, :, 2 * BANK * c : 2 * BANK * (c + 1)].rearrange("g p n -> p g n")
            nc.sync.dma_start(out=w_sb[c][:].bitcast(I32), in_=src.bitcast(I32))

        def load_scales(g):
            for quad in range(4):
                src = W_qkv_scales[:, 4 * quad : 4 * quad + 4, GROUP_COLS * g : GROUP_COLS * (g + 1)]
                nc.sync.dma_start(
                    out=w_scale[g][32 * quad : 32 * quad + 4, :, :].bitcast(I32),
                    in_=src.rearrange("g r n -> r g n").bitcast(I32),
                )

        nc.gpsimd.iota(pos[:], pattern=[[P, TILES]], base=0, channel_multiplier=1, allow_small_or_imprecise_dtypes=True)
        make_identity(nc, ident[:])
        for g in range(GROUPS):
            nc.vector.memset(w_scale[g][:].bitcast(I32), 0)

        load_x(0)
        load_x(1)
        load_words(0)
        for g in range(GROUPS):
            load_scales(g)
        for c in range(1, GROUPS * GROUP_BANKS):
            load_words(c)
        for i in range(2, TILES):
            load_x(i)

        for b in range(8):
            nc.vector.tensor_scalar(
                out=low[:, :, b], in0=pos[:], scalar1=ROPE_BASE ** (-b / HALF) / (2 * math.pi), scalar2=None, op0=ALU.mult
            )
        for m in range(HALF // 8):
            nc.vector.tensor_scalar(
                out=turns[:, :, 8 * m : 8 * m + 8], in0=low[:], scalar1=ROPE_BASE ** (-8 * m / HALF), scalar2=None, op0=ALU.mult
            )
        turns_flat = turns[:].rearrange("p a j -> p (a j)")
        shifts = (0.25, 0.0)
        for w in range(2):
            nc.vector.tensor_scalar(out=whole[:, w, :], in0=turns_flat, scalar1=shifts[w], scalar2=None, op0=ALU.add)
        for w in range(2):
            nc.vector.scalar_tensor_tensor(
                out=frac[:, w, :, :].rearrange("p a j -> p (a j)"),
                in0=turns_flat,
                scalar=shifts[w],
                in1=whole[:, w, :],
                op0=ALU.add,
                op1=ALU.subtract,
            )

        grouped = {}
        codes = {}
        scales = {}
        banks = {}
        rstd = {}

        warm_bank = psum.tile([P, BANK], F32, name="bank")
        warm_act = keep.tile([P, 1], F32)

        def warm_tensor():
            for n in range(3):
                nc.tensor.matmul(warm_bank[:, P * n : P * (n + 1)], lhsT=ident[:], rhs=ident[:], start=True, stop=True)

        def transpose_x(i, copy_out):
            words = x_sb[i][:].bitcast(F32)
            xt = psum.tile([P, BANK], F32, name="bank")
            xt4 = xt[:].rearrange("p (g u r) -> p g u r", g=PASSES, u=2)
            for g in range(PASSES):
                for u in range(2):
                    nc.tensor.transpose(xt4[:, g, u, :], words[:, 256 * g + u : 256 * (g + 1) : 2], ident[:])
            grouped[i] = work.tile([P, D], BF16, name="grouped", align_bytes=64)
            copy_out(
                out=grouped[i][:].bitcast(F32).rearrange("p (g r u) -> p g r u", g=PASSES, u=2),
                in_=xt4.rearrange("p g u r -> p g r u"),
            )

        def quantize_x(i):
            codes[i] = work.tile([P, PASSES * P], U32, name="codes", align_bytes=64)
            scales[i] = work.tile([P, PASSES * P], U8, name="scales", align_bytes=64)
            nc.vector.quantize_mx(out=codes[i][:].bitcast(E5M2X4), scales=scales[i][:], in_=grouped[i][:])

        def inverse_rms(dst, sums):
            nc.scalar.activation(out=dst, in_=sums, func=ACT.Abs_reciprocal_sqrt, scale=1.0 / DH, bias=EPS)

        def project(step):
            i, g = divmod(step, GROUPS)
            sums = work.tile([P, NORMED], F32, name="sums")
            squares = work.tile([P, NORMED, DH], F32, name="squares")
            v_sb = work.tile([P, GROUP_HEADS, DH], F32, name="v_sb")
            rstd[step] = work.tile([P, NORMED], F32, name="rstd")
            order = []
            by_bank = step in (0, TILES * GROUPS - 1)
            for b in range(GROUP_BANKS):
                acc = psum.tile([P, BANK], F32, name="bank")
                banks[step, b] = acc
                for s in range(PASSES):
                    nc.tensor.matmul_mx(
                        out=acc[:],
                        lhsT=codes[i][:, P * s : P * (s + 1)].bitcast(E5M2X4),
                        lhsT_scale=scales[i][:, P * s : P * (s + 1)],
                        rhs=w_sb[GROUP_BANKS * g + b][:, s, :].bitcast(E2M1X4),
                        rhs_scale=w_scale[g][:, s, BANK * b : BANK * (b + 1)],
                        start=(s == 0),
                        stop=(s == PASSES - 1),
                    )
                blocks = acc[:].rearrange("p (n d) -> p n d", d=DH)
                v_slots = []
                first = len(order)
                for n in range(4):
                    head, kind = divmod(4 * b + n, 3)
                    if kind == 2:
                        v_slots.append((n, head))
                    else:
                        unit = GROUP_HEADS * kind + head
                        slot = len(order)
                        order.append(unit)
                        nc.scalar.activation(
                            out=squares[:, slot, :], in_=blocks[:, n, :], func=ACT.Square, accum_out=sums[:, slot : slot + 1]
                        )
                n0, head0 = v_slots[0]
                nc.scalar.copy(out=v_sb[:, head0 : head0 + len(v_slots), :], in_=blocks[:, n0:4:3, :])
                if by_bank:
                    inverse_rms(rstd[step][:, first : len(order)], sums[:, first : len(order)])
            if not by_bank:
                inverse_rms(rstd[step][:], sums[:])
            cols = slice(GROUP_HEADS * DH * g, GROUP_HEADS * DH * (g + 1))
            nc.sync.dma_start(out=v_hbm[i * P : (i + 1) * P, cols], in_=v_sb[:].rearrange("p h d -> p (h d)"))

        def combine(engine, rotated, prods, units):
            halves = prods[:, units, :, :].rearrange("p u w (c j) -> p u w c j", c=2)
            engine.tensor_tensor(
                out=rotated[:, units, :].rearrange("p u (c j) -> p u c j", c=2),
                in0=halves[:, :, 0, :, :],
                in1=halves[:, :, 1, ::-1, :],
                op=ALU.add,
            )

        def rotate(step):
            i, g = divmod(step, GROUPS)
            prods = work.tile([P, NORMED, 2, DH], F32, name="prods")
            rotated = work.tile([P, NORMED, DH], F32, name="rotated")
            slot = 0
            for b in range(GROUP_BANKS):
                blocks = banks[step, b][:].rearrange("p (n d) -> p n d", d=DH)
                for n in range(4):
                    head, kind = divmod(4 * b + n, 3)
                    if kind != 2:
                        unit = GROUP_HEADS * kind + head
                        nc.vector.scalar_tensor_tensor(
                            out=prods[:, unit, :, :],
                            in0=blocks[:, n : n + 1, :].to_broadcast([P, 2, DH]),
                            scalar=rstd[step][:, slot : slot + 1],
                            in1=table[:, i, :, :, :].rearrange("p w c j -> p w (c j)"),
                            op0=ALU.mult,
                            op1=ALU.mult,
                        )
                        slot += 1
            cols = slice(GROUP_HEADS * DH * g, GROUP_HEADS * DH * (g + 1))
            rows = slice(i * P, (i + 1) * P)
            last = step == TILES * GROUPS - 1
            if not last:
                combine(nc.gpsimd, rotated, prods, slice(0, NORMED))
            for kind, dst in enumerate((q_hbm, k_hbm)):
                units = slice(GROUP_HEADS * kind, GROUP_HEADS * (kind + 1))
                if last:
                    combine(nc.vector, rotated, prods, units)
                nc.sync.dma_start(out=dst[rows, cols], in_=rotated[:, units, :].rearrange("p h d -> p (h d)"))

        for w in range(2):
            nc.scalar.activation(out=table[:, :, w, 1, :], in_=frac[:, w, :, :], func=ACT.Sin, scale=2 * math.pi)
        inverse_rms(warm_act[:], pos[:, 0:1])
        warm_tensor()
        transpose_x(0, nc.vector.tensor_copy)
        nc.vector.tensor_copy(out=table[:, :, 0, 0, :], in_=table[:, :, 0, 1, :])
        quantize_x(0)
        transpose_x(1, nc.vector.tensor_copy)
        nc.vector.tensor_scalar(
            out=table[:, :, 1, 0, :], in0=table[:, :, 1, 1, :], scalar1=-1.0, scalar2=None, op0=ALU.mult
        )
        quantize_x(1)
        warm_tensor()

        steps = TILES * GROUPS
        project(0)
        for step in range(steps):
            if step + 1 < steps:
                project(step + 1)
            i, g = divmod(step, GROUPS)
            if g == 0 and i + 2 < TILES:
                transpose_x(i + 2, nc.scalar.copy)
            rotate(step)
            if g == GROUPS - 1 and i + 2 < TILES:
                quantize_x(i + 2)
